import numpy as np
import ml_dtypes


BF16 = ml_dtypes.bfloat16


def bf(x):
    return np.asarray(x, np.float32).astype(BF16)


def f64(x):
    return np.asarray(x).astype(np.float64)


E2M1 = np.array([0.0, 0.5, 1.0, 1.5, 2.0, 3.0, 4.0, 6.0, -0.0, -0.5, -1.0, -1.5, -2.0, -3.0, -4.0, -6.0])


def pack_weight(w, fmt):
    k, n = w.shape
    w = f64(bf(w)).reshape(k // 32, 32, n)
    amax = np.abs(w).max(1)
    if fmt == "e4m3":
        byte = np.frexp(amax)[1] - 1 + 127 - 7
    else:
        mant, ex = np.frexp(amax / 6.0)
        byte = np.where(mant > 0.5, ex, ex - 1) + 127
    byte = np.clip(np.where(amax > 0, byte, 1), 1, 254)
    scaled = (w * np.exp2(127.0 - byte)[:, None, :]).reshape(k, n).astype(np.float32)
    by_word = np.ascontiguousarray(scaled.reshape(k // 512, 128, 4, n).transpose(0, 1, 3, 2))
    if fmt == "e4m3":
        words = by_word.astype(ml_dtypes.float8_e4m3fn).view(np.uint8)
    else:
        c = by_word.astype(ml_dtypes.float4_e2m1fn).view(np.uint8) & 0xF
        words = c[..., 0::2] | (c[..., 1::2] << 4)
    return np.ascontiguousarray(words), np.ascontiguousarray(byte.astype(np.uint8).reshape(k // 512, 16, n))


def unpack_weight(words, scales, fmt):
    g, p, n, _ = words.shape
    if fmt == "e4m3":
        vals = np.ascontiguousarray(words).view(ml_dtypes.float8_e4m3fn).astype(np.float64)
    else:
        nib = np.empty((g, p, n, 4), np.uint8)
        nib[..., 0::2] = words & 0xF
        nib[..., 1::2] = words >> 4
        vals = E2M1[nib]
    vals = vals * np.repeat(np.exp2(scales.astype(np.float64) - 127.0), 8, axis=1)[..., None]
    return vals.transpose(0, 1, 3, 2).reshape(g * 512, n)

def pack4(w):
    words, scales = pack_weight(w, "e2m1")
    return words.reshape(words.shape[0], 128, -1), scales


def unpack4(words, scales):
    return unpack_weight(words.reshape(words.shape[0], 128, -1, 2), scales, "e2m1")


def kspread(k):
    return np.exp2(np.repeat(np.random.randint(-6, 7, k // 32), 32).astype(np.float64))


B, S, D, E, H = 2, 512, 4096, 3072, 2
DH = E // H
ROPE_BASE = 10000.0


def rope_tables():
    inv_freq = 1.0 / (ROPE_BASE ** (np.arange(0, DH, 2) / DH))
    freqs = np.arange(S)[:, None] * inv_freq[None, :]
    emb = np.concatenate([freqs, freqs], axis=-1)
    return np.cos(emb), np.sin(emb)


def rotate(y, cos, sin):
    y1, y2 = y[..., :DH], y[..., DH:]
    return np.concatenate([y1 * cos - y2 * sin, y2 * cos + y1 * sin], axis=-1)


def setup_inputs():
    s = kspread(D)
    cos, sin = rope_tables()
    x = np.random.standard_normal((B, S, D)) * s
    x_words, x_scales = pack4(np.ascontiguousarray(x.reshape(B * S, D).T))
    wq_words, wq_scales = pack4(np.random.standard_normal((D, E)) / np.sqrt(D) / s[:, None])
    wk_words, wk_scales = pack4(np.random.standard_normal((D, E)) / np.sqrt(D) / s[:, None])
    return {"x_words": x_words, "x_scales": x_scales,
            "wq_words": wq_words, "wq_scales": wq_scales,
            "wk_words": wk_words, "wk_scales": wk_scales,
            "cos": bf(cos), "sin": bf(sin)}


def reference(x_words, x_scales, wq_words, wq_scales, wk_words, wk_scales, cos, sin):
    xq = unpack4(x_words, x_scales).T.reshape(B, S, D)
    q = xq @ unpack4(wq_words, wq_scales)
    k = xq @ unpack4(wk_words, wk_scales)
    c, sn = f64(cos), f64(sin)
    q_rot = rotate(q, c, sn).reshape(B, S, H, DH).transpose(0, 2, 1, 3)
    k_rot = rotate(k, c, sn).reshape(B, S, H, DH).transpose(0, 2, 1, 3)
    return q_rot, k_rot

@@ -1,0 +1,225 @@
+from contextlib import ExitStack
+
+import concourse.mybir as mybir
+
+F32 = mybir.dt.float32
+BF16 = mybir.dt.bfloat16
+I32 = mybir.dt.int32
+U8 = mybir.dt.uint8
+FP4X4 = mybir.dt.float4_e2m1fn_x4
+MULT = mybir.AluOpType.mult
+ADD = mybir.AluOpType.add
+
+P = 128
+BATCH, SEQ, D, E = 2, 512, 4096, 3072
+TOKENS = BATCH * SEQ
+DH = E // 2
+PASSES = D // 512
+W = 512
+TOKEN_TILES = TOKENS // P
+POS_TILES = SEQ // P
+BANKS = 8
+RING = 6
+WARMUP = 40
+GROUPS = ((0, 1), (1, 4), (4, 8))
+TAIL_WIDTHS = (256, 128, 128)
+
+FLOPS = 2 * TOKENS * D * 2 * E
+
+
+def load_codes(nc, g0, g1, codes, words, c0, cols):
+    nc.sync.dma_start(
+        out=codes[:].bitcast(I32),
+        in_=words[g0:g1, :, 2 * c0 : 2 * (c0 + cols)].rearrange("g p c -> p g c").bitcast(I32),
+    )
+
+
+def load_scales(nc, g0, g1, planes, scales, c0, cols):
+    for q in range(4):
+        nc.sync.dma_start(
+            out=planes[32 * q : 32 * q + 4, :, :].bitcast(I32),
+            in_=scales[g0:g1, 4 * q : 4 * q + 4, c0 : c0 + cols].rearrange("g r n -> r g n").bitcast(I32),
+        )
+
+
+def tile_multiheadattention_pa_kernel(
+    tc, x_words, x_scales, wq_words, wq_scales, wk_words, wk_scales, cos, sin, out_0, out_1
+):
+    nc = tc.nc
+    weights = ((wq_words, wq_scales, out_0), (wk_words, wk_scales, out_1))
+    units = [(cb, m) for cb in range(DH // W) for m in range(2)]
+
+    with ExitStack() as ctx:
+        keep = ctx.enter_context(tc.tile_pool(name="keep", bufs=1))
+        first = ctx.enter_context(tc.tile_pool(name="first", bufs=10))
+        second = ctx.enter_context(tc.tile_pool(name="second", bufs=3))
+        psum = ctx.enter_context(tc.psum_pool(name="psum", bufs=1))
+        ctx.enter_context(tc.manual_schedule())
+
+        def bank(i):
+            acc = psum.tile([P, W], F32, name="bank%d" % (i % BANKS))
+            return acc
+
+        zero = keep.tile([P, P], BF16, name="zero")
+        x_parts, w0_parts = [], []
+        for g0, g1 in GROUPS:
+            n = g1 - g0
+            xc = keep.tile([P, n, 2 * TOKENS], U8, name="xc%d" % (g0), align_bytes=256)
+            xs = keep.tile([P, n, TOKENS], U8, name="xs%d" % (g0), align_bytes=256)
+            wc = keep.tile([P, n, 2 * W], U8, name="w0c%d" % (g0), align_bytes=256)
+            ws = keep.tile([P, n, W], U8, name="w0s%d" % (g0), align_bytes=256)
+            x_parts.append((g0, g1, xc, xs))
+            w0_parts.append((g0, g1, wc, ws))
+        ring = []
+        for i in range(RING):
+            wc = keep.tile([P, PASSES, 2 * W], U8, name="wc%d" % (i), align_bytes=256)
+            ws = keep.tile([P, PASSES, W], U8, name="ws%d" % (i), align_bytes=256)
+            ring.append((wc, ws))
+        tables = []
+        for i in range(2):
+            cos_sb = keep.tile([P, POS_TILES, W], BF16, name="cos%d" % (i), align_bytes=64)
+            sin_sb = keep.tile([P, POS_TILES, W], BF16, name="sin%d" % (i), align_bytes=64)
+            tables.append((cos_sb, sin_sb))
+
+        def parts_of(piece):
+            if piece == 0:
+                return w0_parts
+            wc, ws = ring[(piece - 1) % RING]
+            return [(0, PASSES, wc, ws)]
+
+        def load_piece(piece):
+            cb, m = units[piece // 2]
+            words, scales, unused_out = weights[m]
+            c0 = (piece % 2) * DH + cb * W
+            for g0, g1, codes, planes in parts_of(piece):
+                load_codes(nc, g0, g1, codes, words, c0, W)
+                load_scales(nc, g0, g1, planes, scales, c0, W)
+
+        def load_tables(cb):
+            cos_sb, sin_sb = tables[cb % 2]
+            for sb, hbm in ((cos_sb, cos), (sin_sb, sin)):
+                nc.sync.dma_start(
+                    out=sb[:], in_=hbm.rearrange("(t p) c -> p t c", p=P)[:, :, cb * W : (cb + 1) * W]
+                )
+
+        def mx(acc, width, tt, piece, g, c0=0):
+            for g0, g1, codes, planes in x_parts:
+                if g0 <= g < g1:
+                    lhsT = codes[:, g - g0, 2 * P * tt : 2 * P * (tt + 1)].bitcast(FP4X4)
+                    lhsT_scale = planes[:, g - g0, P * tt : P * (tt + 1)]
+            for g0, g1, codes, planes in parts_of(piece):
+                if g0 <= g < g1:
+                    rhs = codes[:, g - g0, 2 * c0 : 2 * (c0 + width)].bitcast(FP4X4)
+                    rhs_scale = planes[:, g - g0, c0 : c0 + width]
+            nc.tensor.matmul_mx(
+                out=acc[:, 0:width],
+                lhsT=lhsT,
+                lhsT_scale=lhsT_scale,
+                rhs=rhs,
+                rhs_scale=rhs_scale,
+                start=(g == 0),
+                stop=(g == PASSES - 1),
+            )
+
+        def head0_products(acc, width, tt, cb, c0=0):
+            cos_sb, sin_sb = tables[cb % 2]
+            cols = slice(c0, c0 + width)
+            a = first.tile([P, 2, W], F32, name="a")
+            nc.vector.tensor_tensor(
+                out=a[:, 0, 0:width], in0=acc[:, 0:width], in1=cos_sb[:, tt % POS_TILES, cols], op=MULT
+            )
+            nc.vector.tensor_tensor(
+                out=a[:, 1, 0:width], in0=acc[:, 0:width], in1=sin_sb[:, tt % POS_TILES, cols], op=MULT
+            )
+            return a
+
+        def head1_products(acc, width, tt, cb, c0=0):
+            cos_sb, sin_sb = tables[cb % 2]
+            cols = slice(c0, c0 + width)
+            b = second.tile([P, 2, W], F32, name="b")
+            nc.vector.scalar_tensor_tensor(
+                out=b[:, 0, 0:width],
+                in0=acc[:, 0:width],
+                scalar=-1.0,
+                in1=sin_sb[:, tt % POS_TILES, cols],
+                op0=MULT,
+                op1=MULT,
+            )
+            nc.vector.tensor_tensor(
+                out=b[:, 1, 0:width], in0=acc[:, 0:width], in1=cos_sb[:, tt % POS_TILES, cols], op=MULT
+            )
+            return b
+
+        def add_and_store(engine, a, b, width, tt, cb, m, c0=0):
+            engine.tensor_tensor(out=a[:, :, 0:width], in0=a[:, :, 0:width], in1=b[:, :, 0:width], op=ADD)
+            hbm = weights[m][2]
+            pos = (tt % POS_TILES) * P
+            nc.scalar.dma_start(
+                out=hbm[tt // POS_TILES, :, pos : pos + P, cb * W + c0 : cb * W + c0 + width].rearrange(
+                    "h p c -> p h c"
+                ),
+                in_=a[:, :, 0:width],
+            )
+
+        nc.gpsimd.memset(zero[:], 0.0)
+        for (g0, g1, wc, ws), (xg0, xg1, xc, xs) in zip(w0_parts, x_parts):
+            nc.vector.memset(ws[:].bitcast(I32), 0)
+            nc.vector.memset(xs[:].bitcast(I32), 0)
+        for wc, ws in ring:
+            nc.vector.memset(ws[:].bitcast(I32), 0)
+        for (g0, g1, wc, ws), (xg0, xg1, xc, xs) in zip(w0_parts, x_parts):
+            load_codes(nc, g0, g1, wc, wq_words, 0, W)
+            load_codes(nc, g0, g1, xc, x_words, 0, TOKENS)
+            load_scales(nc, g0, g1, ws, wq_scales, 0, W)
+            load_scales(nc, g0, g1, xs, x_scales, 0, TOKENS)
+        load_tables(0)
+        for piece in range(1, 4):
+            load_piece(piece)
+        load_tables(1)
+        for piece in range(4, RING + 1):
+            load_piece(piece)
+
+        warm = bank(BANKS - 1)
+        for i in range(WARMUP):
+            nc.tensor.matmul(out=warm[:, 0:P], lhsT=zero[:], rhs=zero[:], start=True, stop=True)
+
+        accs = []
+        for tt in range(TOKEN_TILES):
+            accs.append(bank(tt))
+        for g in range(PASSES):
+            for tt in range(TOKEN_TILES):
+                mx(accs[tt], W, tt, 0, g)
+        firsts = []
+        for tt in range(TOKEN_TILES):
+            firsts.append(head0_products(accs[tt], W, tt, 0))
+        for tt in range(TOKEN_TILES):
+            acc = bank(tt)
+            for g in range(PASSES):
+                mx(acc, W, tt, 1, g)
+            b = head1_products(acc, W, tt, 0)
+            add_and_store(nc.gpsimd, firsts[tt], b, W, tt, 0, 0)
+
+        slot = 0
+        for u in range(1, len(units)):
+            cb, m = units[u]
+            for piece in (2 * u + RING - 2, 2 * u + RING - 1):
+                if RING < piece < 2 * len(units):
+                    load_piece(piece)
+            if m == 0 and cb + 1 == 2:
+                load_tables(2)
+            for tt in range(TOKEN_TILES):
+                last = u == len(units) - 1 and tt == TOKEN_TILES - 1
+                c0 = 0
+                for width in TAIL_WIDTHS if last else (W,):
+                    acc0 = bank(slot)
+                    for g in range(PASSES):
+                        mx(acc0, width, tt, 2 * u, g, c0)
+                    a = head0_products(acc0, width, tt, cb, c0)
+                    acc1 = bank(slot + 1)
+                    for g in range(PASSES):
+                        mx(acc1, width, tt, 2 * u + 1, g, c0)
+                    b = head1_products(acc1, width, tt, cb, c0)
+                    end = c0 + width == W and last
+                    add_and_store(nc.vector if end else nc.gpsimd, a, b, width, tt, cb, m, c0)
+                    slot += 2
+                    c0 += width

@@ -20,8 +20,10 @@ TOKEN_TILES = TOKENS // P
 POS_TILES = SEQ // P
 BANKS = 8
 RING = 6
-WARMUP = 40
-GROUPS = ((0, 1), (1, 4), (4, 8))
+WARMUP = 36
+CODE_GROUPS = ((0, 1), (1, 2), (2, 4), (4, 8))
+SCALE_GROUPS = ((0, 2), (2, 8))
+HEAD_TOKENS = 256
 TAIL_WIDTHS = (256, 128, 128)
 
 FLOPS = 2 * TOKENS * D * 2 * E
@@ -29,7 +31,7 @@ FLOPS = 2 * TOKENS * D * 2 * E
 
 def load_codes(nc, g0, g1, codes, words, c0, cols):
     nc.sync.dma_start(
-        out=codes[:].bitcast(I32),
+        out=codes.bitcast(I32),
         in_=words[g0:g1, :, 2 * c0 : 2 * (c0 + cols)].rearrange("g p c -> p g c").bitcast(I32),
     )
 
@@ -61,15 +63,17 @@ def tile_multiheadattention_pa_kernel(
             return acc
 
         zero = keep.tile([P, P], BF16, name="zero")
-        x_parts, w0_parts = [], []
-        for g0, g1 in GROUPS:
-            n = g1 - g0
-            xc = keep.tile([P, n, 2 * TOKENS], U8, name="xc%d" % (g0), align_bytes=256)
-            xs = keep.tile([P, n, TOKENS], U8, name="xs%d" % (g0), align_bytes=256)
-            wc = keep.tile([P, n, 2 * W], U8, name="w0c%d" % (g0), align_bytes=256)
-            ws = keep.tile([P, n, W], U8, name="w0s%d" % (g0), align_bytes=256)
-            x_parts.append((g0, g1, xc, xs))
-            w0_parts.append((g0, g1, wc, ws))
+        x_codes, x_planes, w0_codes, w0_planes = [], [], [], []
+        for g0, g1 in CODE_GROUPS:
+            xc = keep.tile([P, g1 - g0, 2 * TOKENS], U8, name="xc%d" % g0, align_bytes=256)
+            wc = keep.tile([P, g1 - g0, 2 * W], U8, name="w0c%d" % g0, align_bytes=256)
+            x_codes.append((g0, g1, xc))
+            w0_codes.append((g0, g1, wc))
+        for g0, g1 in SCALE_GROUPS:
+            xs = keep.tile([P, g1 - g0, TOKENS], U8, name="xs%d" % g0, align_bytes=256)
+            ws = keep.tile([P, g1 - g0, W], U8, name="w0s%d" % g0, align_bytes=256)
+            x_planes.append((g0, g1, xs))
+            w0_planes.append((g0, g1, ws))
         ring = []
         for i in range(RING):
             wc = keep.tile([P, PASSES, 2 * W], U8, name="wc%d" % (i), align_bytes=256)
@@ -83,17 +87,23 @@ def tile_multiheadattention_pa_kernel(
 
         def parts_of(piece):
             if piece == 0:
-                return w0_parts
+                return w0_codes, w0_planes
             wc, ws = ring[(piece - 1) % RING]
-            return [(0, PASSES, wc, ws)]
+            return [(0, PASSES, wc)], [(0, PASSES, ws)]
+
+        def pass_of(groups, g, first_byte, n):
+            for g0, g1, t in groups:
+                if g0 <= g < g1:
+                    return t[:, g - g0, first_byte : first_byte + n]
+            raise ValueError("no such pass")
 
         def load_piece(piece):
             cb, m = units[piece // 2]
             words, scales, unused_out = weights[m]
             c0 = (piece % 2) * DH + cb * W
-            for g0, g1, codes, planes in parts_of(piece):
-                load_codes(nc, g0, g1, codes, words, c0, W)
-                load_scales(nc, g0, g1, planes, scales, c0, W)
+            wc, ws = ring[(piece - 1) % RING]
+            load_codes(nc, 0, PASSES, wc[:], words, c0, W)
+            load_scales(nc, 0, PASSES, ws, scales, c0, W)
 
         def load_tables(cb):
             cos_sb, sin_sb = tables[cb % 2]
@@ -103,20 +113,13 @@ def tile_multiheadattention_pa_kernel(
                 )
 
         def mx(acc, width, tt, piece, g, c0=0):
-            for g0, g1, codes, planes in x_parts:
-                if g0 <= g < g1:
-                    lhsT = codes[:, g - g0, 2 * P * tt : 2 * P * (tt + 1)].bitcast(FP4X4)
-                    lhsT_scale = planes[:, g - g0, P * tt : P * (tt + 1)]
-            for g0, g1, codes, planes in parts_of(piece):
-                if g0 <= g < g1:
-                    rhs = codes[:, g - g0, 2 * c0 : 2 * (c0 + width)].bitcast(FP4X4)
-                    rhs_scale = planes[:, g - g0, c0 : c0 + width]
+            w_codes, w_planes = parts_of(piece)
             nc.tensor.matmul_mx(
                 out=acc[:, 0:width],
-                lhsT=lhsT,
-                lhsT_scale=lhsT_scale,
-                rhs=rhs,
-                rhs_scale=rhs_scale,
+                lhsT=pass_of(x_codes, g, 2 * P * tt, 2 * P).bitcast(FP4X4),
+                lhsT_scale=pass_of(x_planes, g, P * tt, P),
+                rhs=pass_of(w_codes, g, 2 * c0, 2 * width).bitcast(FP4X4),
+                rhs_scale=pass_of(w_planes, g, c0, width),
                 start=(g == 0),
                 stop=(g == PASSES - 1),
             )
@@ -162,16 +165,30 @@ def tile_multiheadattention_pa_kernel(
             )
 
         nc.gpsimd.memset(zero[:], 0.0)
-        for (g0, g1, wc, ws), (xg0, xg1, xc, xs) in zip(w0_parts, x_parts):
-            nc.vector.memset(ws[:].bitcast(I32), 0)
-            nc.vector.memset(xs[:].bitcast(I32), 0)
+        for i in range(len(SCALE_GROUPS)):
+            nc.vector.memset(w0_planes[i][2][:].bitcast(I32), 0)
+            nc.vector.memset(x_planes[i][2][:].bitcast(I32), 0)
         for wc, ws in ring:
             nc.vector.memset(ws[:].bitcast(I32), 0)
-        for (g0, g1, wc, ws), (xg0, xg1, xc, xs) in zip(w0_parts, x_parts):
-            load_codes(nc, g0, g1, wc, wq_words, 0, W)
-            load_codes(nc, g0, g1, xc, x_words, 0, TOKENS)
+        def load_start_codes(i, c0, c1):
+            g0, g1, wc = w0_codes[i]
+            xc = x_codes[i][2]
+            if c0 == 0:
+                load_codes(nc, g0, g1, wc[:], wq_words, 0, W)
+            load_codes(nc, g0, g1, xc[:, :, 2 * c0 : 2 * c1], x_words, c0, c1 - c0)
+
+        def load_start_scales(i):
+            g0, g1, ws = w0_planes[i]
             load_scales(nc, g0, g1, ws, wq_scales, 0, W)
-            load_scales(nc, g0, g1, xs, x_scales, 0, TOKENS)
+            load_scales(nc, g0, g1, x_planes[i][2], x_scales, 0, TOKENS)
+
+        load_start_codes(0, 0, HEAD_TOKENS)
+        load_start_scales(0)
+        load_start_codes(0, HEAD_TOKENS, TOKENS)
+        load_start_codes(1, 0, TOKENS)
+        load_start_codes(2, 0, TOKENS)
+        load_start_scales(1)
+        load_start_codes(3, 0, TOKENS)
         load_tables(0)
         for piece in range(1, 4):
             load_piece(piece)
@@ -219,7 +236,7 @@ def tile_multiheadattention_pa_kernel(
                     for g in range(PASSES):
                         mx(acc1, width, tt, 2 * u + 1, g, c0)
                     b = head1_products(acc1, width, tt, cb, c0)
-                    end = c0 + width == W and last
+                    end = last and c0 >= TAIL_WIDTHS[0]
                     add_and_store(nc.vector if end else nc.gpsimd, a, b, width, tt, cb, m, c0)
                     slot += 2
                     c0 += width

@@ -21,8 +21,8 @@ POS_TILES = SEQ // P
 BANKS = 8
 RING = 6
 WARMUP = 36
-CODE_GROUPS = ((0, 1), (1, 2), (2, 4), (4, 8))
-SCALE_GROUPS = ((0, 2), (2, 8))
+CODE_GROUPS = ((0, 1), (1, 4), (4, 6), (6, 8))
+SCALE_GROUPS = ((0, 2), (2, 4), (4, 8))
 HEAD_TOKENS = 256
 TAIL_WIDTHS = (256, 128, 128)
 
@@ -37,10 +37,10 @@ def load_codes(nc, g0, g1, codes, words, c0, cols):
 
 
 def load_scales(nc, g0, g1, planes, scales, c0, cols):
-    for q in range(4):
+    for r in range(4):
         nc.sync.dma_start(
-            out=planes[32 * q : 32 * q + 4, :, :].bitcast(I32),
-            in_=scales[g0:g1, 4 * q : 4 * q + 4, c0 : c0 + cols].rearrange("g r n -> r g n").bitcast(I32),
+            out=planes[r:P:32, :, :].bitcast(I32),
+            in_=scales[g0:g1, r:16:4, c0 : c0 + cols].rearrange("g q n -> q g n").bitcast(I32),
         )
 
 
@@ -186,8 +186,9 @@ def tile_multiheadattention_pa_kernel(
         load_start_scales(0)
         load_start_codes(0, HEAD_TOKENS, TOKENS)
         load_start_codes(1, 0, TOKENS)
-        load_start_codes(2, 0, TOKENS)
         load_start_scales(1)
+        load_start_codes(2, 0, TOKENS)
+        load_start_scales(2)
         load_start_codes(3, 0, TOKENS)
         load_tables(0)
         for piece in range(1, 4):

@@ -25,6 +25,8 @@ CODE_GROUPS = ((0, 1), (1, 4), (4, 6), (6, 8))
 SCALE_GROUPS = ((0, 2), (2, 4), (4, 8))
 HEAD_TOKENS = 256
 TAIL_WIDTHS = (256, 128, 128)
+DIRECT = 3
+SUB = mybir.AluOpType.subtract
 
 FLOPS = 2 * TOKENS * D * 2 * E
 
@@ -53,8 +55,9 @@ def tile_multiheadattention_pa_kernel(
 
     with ExitStack() as ctx:
         keep = ctx.enter_context(tc.tile_pool(name="keep", bufs=1))
-        first = ctx.enter_context(tc.tile_pool(name="first", bufs=10))
-        second = ctx.enter_context(tc.tile_pool(name="second", bufs=3))
+        heads = ctx.enter_context(tc.tile_pool(name="heads", bufs=8))
+        first = ctx.enter_context(tc.tile_pool(name="first", bufs=5))
+        second = ctx.enter_context(tc.tile_pool(name="second", bufs=4))
         psum = ctx.enter_context(tc.psum_pool(name="psum", bufs=1))
         ctx.enter_context(tc.manual_schedule())
 
@@ -155,14 +158,41 @@ def tile_multiheadattention_pa_kernel(
 
         def add_and_store(engine, a, b, width, tt, cb, m, c0=0):
             engine.tensor_tensor(out=a[:, :, 0:width], in0=a[:, :, 0:width], in1=b[:, :, 0:width], op=ADD)
+            store(a, width, tt, cb, m, c0)
+
+        def store(a, width, tt, cb, m, c0=0):
             hbm = weights[m][2]
             pos = (tt % POS_TILES) * P
-            nc.scalar.dma_start(
+            nc.sync.dma_start(
                 out=hbm[tt // POS_TILES, :, pos : pos + P, cb * W + c0 : cb * W + c0 + width].rearrange(
                     "h p c -> p h c"
                 ),
                 in_=a[:, :, 0:width],
             )
+
+        waiting = []
+
+        def finish_head0():
+            for a, b, tt, cb, m in waiting:
+                nc.vector.tensor_tensor(out=a[:, 0, :], in0=a[:, 0, :], in1=b[:, 1, :], op=SUB)
+
+        def finish_head1():
+            for a, b, tt, cb, m in waiting:
+                nc.vector.tensor_tensor(out=a[:, 1, :], in0=a[:, 1, :], in1=b[:, 0, :], op=ADD)
+                store(a, W, tt, cb, m)
+            waiting.clear()
+
+        def rotate(both, tt, cb, m):
+            cos_sb, sin_sb = tables[cb % 2]
+            cos_tt = cos_sb[:, tt % POS_TILES, :].unsqueeze(1).to_broadcast([P, 2, W])
+            sin_tt = sin_sb[:, tt % POS_TILES, :].unsqueeze(1).to_broadcast([P, 2, W])
+            a = first.tile([P, 2, W], F32, name="a")
+            b = second.tile([P, 2, W], F32, name="b")
+            nc.vector.tensor_tensor(out=a[:], in0=both[:], in1=cos_tt, op=MULT)
+            finish_head0()
+            nc.vector.tensor_tensor(out=b[:], in0=both[:], in1=sin_tt, op=MULT)
+            finish_head1()
+            waiting.append((a, b, tt, cb, m))
 
         nc.gpsimd.memset(zero[:], 0.0)
         for i in range(len(SCALE_GROUPS)):
@@ -193,9 +223,6 @@ def tile_multiheadattention_pa_kernel(
         load_tables(0)
         for piece in range(1, 4):
             load_piece(piece)
-        load_tables(1)
-        for piece in range(4, RING + 1):
-            load_piece(piece)
 
         warm = bank(BANKS - 1)
         for i in range(WARMUP):
@@ -207,15 +234,20 @@ def tile_multiheadattention_pa_kernel(
         for g in range(PASSES):
             for tt in range(TOKEN_TILES):
                 mx(accs[tt], W, tt, 0, g)
-        firsts = []
+        pairs = []
         for tt in range(TOKEN_TILES):
-            firsts.append(head0_products(accs[tt], W, tt, 0))
+            both = heads.tile([P, 2, W], F32, name="both")
+            nc.scalar.copy(out=both[:, 0, :], in_=accs[tt][:])
+            pairs.append(both)
         for tt in range(TOKEN_TILES):
             acc = bank(tt)
             for g in range(PASSES):
                 mx(acc, W, tt, 1, g)
-            b = head1_products(acc, W, tt, 0)
-            add_and_store(nc.gpsimd, firsts[tt], b, W, tt, 0, 0)
+            nc.scalar.copy(out=pairs[tt][:, 1, :], in_=acc[:])
+            rotate(pairs[tt], tt, 0, 0)
+            if 4 + tt // 2 <= RING and tt % 2 == 1:
+                load_piece(4 + tt // 2)
+        load_tables(1)
 
         slot = 0
         for u in range(1, len(units)):
@@ -227,6 +259,18 @@ def tile_multiheadattention_pa_kernel(
                 load_tables(2)
             for tt in range(TOKEN_TILES):
                 last = u == len(units) - 1 and tt == TOKEN_TILES - 1
+                if u < len(units) - 1 or tt < TOKEN_TILES - DIRECT:
+                    both = heads.tile([P, 2, W], F32, name="both")
+                    for h in range(2):
+                        acc = bank(slot + h)
+                        for g in range(PASSES):
+                            mx(acc, W, tt, 2 * u + h, g)
+                        nc.scalar.copy(out=both[:, h, :], in_=acc[:])
+                    rotate(both, tt, cb, m)
+                    slot += 2
+                    continue
+                finish_head0()
+                finish_head1()
                 c0 = 0
                 for width in TAIL_WIDTHS if last else (W,):
                     acc0 = bank(slot)

from contextlib import ExitStack

import concourse.mybir as mybir

F32 = mybir.dt.float32
BF16 = mybir.dt.bfloat16
I32 = mybir.dt.int32
U8 = mybir.dt.uint8
FP4X4 = mybir.dt.float4_e2m1fn_x4
MULT = mybir.AluOpType.mult
ADD = mybir.AluOpType.add

P = 128
BATCH, SEQ, D, E = 2, 512, 4096, 3072
TOKENS = BATCH * SEQ
DH = E // 2
PASSES = D // 512
W = 512
TOKEN_TILES = TOKENS // P
POS_TILES = SEQ // P
BANKS = 8
RING = 6
WARMUP = 36
CODE_GROUPS = ((0, 1), (1, 4), (4, 6), (6, 8))
SCALE_GROUPS = ((0, 2), (2, 4), (4, 8))
HEAD_TOKENS = 256
TAIL_WIDTHS = (256, 128, 128)
DIRECT = 3
SUB = mybir.AluOpType.subtract

FLOPS = 2 * TOKENS * D * 2 * E


def load_codes(nc, g0, g1, codes, words, c0, cols):
    nc.sync.dma_start(
        out=codes.bitcast(I32),
        in_=words[g0:g1, :, 2 * c0 : 2 * (c0 + cols)].rearrange("g p c -> p g c").bitcast(I32),
    )


def load_scales(nc, g0, g1, planes, scales, c0, cols):
    for r in range(4):
        nc.sync.dma_start(
            out=planes[r:P:32, :, :].bitcast(I32),
            in_=scales[g0:g1, r:16:4, c0 : c0 + cols].rearrange("g q n -> q g n").bitcast(I32),
        )


def tile_multiheadattention_pa_kernel(
    tc, x_words, x_scales, wq_words, wq_scales, wk_words, wk_scales, cos, sin, out_0, out_1
):
    nc = tc.nc
    weights = ((wq_words, wq_scales, out_0), (wk_words, wk_scales, out_1))
    units = [(cb, m) for cb in range(DH // W) for m in range(2)]

    with ExitStack() as ctx:
        keep = ctx.enter_context(tc.tile_pool(name="keep", bufs=1))
        heads = ctx.enter_context(tc.tile_pool(name="heads", bufs=8))
        first = ctx.enter_context(tc.tile_pool(name="first", bufs=5))
        second = ctx.enter_context(tc.tile_pool(name="second", bufs=4))
        psum = ctx.enter_context(tc.psum_pool(name="psum", bufs=1))
        ctx.enter_context(tc.manual_schedule())

        def bank(i):
            acc = psum.tile([P, W], F32, name="bank%d" % (i % BANKS))
            return acc

        zero = keep.tile([P, P], BF16, name="zero")
        x_codes, x_planes, w0_codes, w0_planes = [], [], [], []
        for g0, g1 in CODE_GROUPS:
            xc = keep.tile([P, g1 - g0, 2 * TOKENS], U8, name="xc%d" % g0, align_bytes=256)
            wc = keep.tile([P, g1 - g0, 2 * W], U8, name="w0c%d" % g0, align_bytes=256)
            x_codes.append((g0, g1, xc))
            w0_codes.append((g0, g1, wc))
        for g0, g1 in SCALE_GROUPS:
            xs = keep.tile([P, g1 - g0, TOKENS], U8, name="xs%d" % g0, align_bytes=256)
            ws = keep.tile([P, g1 - g0, W], U8, name="w0s%d" % g0, align_bytes=256)
            x_planes.append((g0, g1, xs))
            w0_planes.append((g0, g1, ws))
        ring = []
        for i in range(RING):
            wc = keep.tile([P, PASSES, 2 * W], U8, name="wc%d" % (i), align_bytes=256)
            ws = keep.tile([P, PASSES, W], U8, name="ws%d" % (i), align_bytes=256)
            ring.append((wc, ws))
        tables = []
        for i in range(2):
            cos_sb = keep.tile([P, POS_TILES, W], BF16, name="cos%d" % (i), align_bytes=64)
            sin_sb = keep.tile([P, POS_TILES, W], BF16, name="sin%d" % (i), align_bytes=64)
            tables.append((cos_sb, sin_sb))

        def parts_of(piece):
            if piece == 0:
                return w0_codes, w0_planes
            wc, ws = ring[(piece - 1) % RING]
            return [(0, PASSES, wc)], [(0, PASSES, ws)]

        def pass_of(groups, g, first_byte, n):
            for g0, g1, t in groups:
                if g0 <= g < g1:
                    return t[:, g - g0, first_byte : first_byte + n]
            raise ValueError("no such pass")

        def load_piece(piece):
            cb, m = units[piece // 2]
            words, scales, unused_out = weights[m]
            c0 = (piece % 2) * DH + cb * W
            wc, ws = ring[(piece - 1) % RING]
            load_codes(nc, 0, PASSES, wc[:], words, c0, W)
            load_scales(nc, 0, PASSES, ws, scales, c0, W)

        def load_tables(cb):
            cos_sb, sin_sb = tables[cb % 2]
            for sb, hbm in ((cos_sb, cos), (sin_sb, sin)):
                nc.sync.dma_start(
                    out=sb[:], in_=hbm.rearrange("(t p) c -> p t c", p=P)[:, :, cb * W : (cb + 1) * W]
                )

        def mx(acc, width, tt, piece, g, c0=0):
            w_codes, w_planes = parts_of(piece)
            nc.tensor.matmul_mx(
                out=acc[:, 0:width],
                lhsT=pass_of(x_codes, g, 2 * P * tt, 2 * P).bitcast(FP4X4),
                lhsT_scale=pass_of(x_planes, g, P * tt, P),
                rhs=pass_of(w_codes, g, 2 * c0, 2 * width).bitcast(FP4X4),
                rhs_scale=pass_of(w_planes, g, c0, width),
                start=(g == 0),
                stop=(g == PASSES - 1),
            )

        def head0_products(acc, width, tt, cb, c0=0):
            cos_sb, sin_sb = tables[cb % 2]
            cols = slice(c0, c0 + width)
            a = first.tile([P, 2, W], F32, name="a")
            nc.vector.tensor_tensor(
                out=a[:, 0, 0:width], in0=acc[:, 0:width], in1=cos_sb[:, tt % POS_TILES, cols], op=MULT
            )
            nc.vector.tensor_tensor(
                out=a[:, 1, 0:width], in0=acc[:, 0:width], in1=sin_sb[:, tt % POS_TILES, cols], op=MULT
            )
            return a

        def head1_products(acc, width, tt, cb, c0=0):
            cos_sb, sin_sb = tables[cb % 2]
            cols = slice(c0, c0 + width)
            b = second.tile([P, 2, W], F32, name="b")
            nc.vector.scalar_tensor_tensor(
                out=b[:, 0, 0:width],
                in0=acc[:, 0:width],
                scalar=-1.0,
                in1=sin_sb[:, tt % POS_TILES, cols],
                op0=MULT,
                op1=MULT,
            )
            nc.vector.tensor_tensor(
                out=b[:, 1, 0:width], in0=acc[:, 0:width], in1=cos_sb[:, tt % POS_TILES, cols], op=MULT
            )
            return b

        def add_and_store(engine, a, b, width, tt, cb, m, c0=0):
            engine.tensor_tensor(out=a[:, :, 0:width], in0=a[:, :, 0:width], in1=b[:, :, 0:width], op=ADD)
            store(a, width, tt, cb, m, c0)

        def store(a, width, tt, cb, m, c0=0):
            hbm = weights[m][2]
            pos = (tt % POS_TILES) * P
            nc.sync.dma_start(
                out=hbm[tt // POS_TILES, :, pos : pos + P, cb * W + c0 : cb * W + c0 + width].rearrange(
                    "h p c -> p h c"
                ),
                in_=a[:, :, 0:width],
            )

        waiting = []

        def finish_head0():
            for a, b, tt, cb, m in waiting:
                nc.vector.tensor_tensor(out=a[:, 0, :], in0=a[:, 0, :], in1=b[:, 1, :], op=SUB)

        def finish_head1():
            for a, b, tt, cb, m in waiting:
                nc.vector.tensor_tensor(out=a[:, 1, :], in0=a[:, 1, :], in1=b[:, 0, :], op=ADD)
                store(a, W, tt, cb, m)
            waiting.clear()

        def rotate(both, tt, cb, m):
            cos_sb, sin_sb = tables[cb % 2]
            cos_tt = cos_sb[:, tt % POS_TILES, :].unsqueeze(1).to_broadcast([P, 2, W])
            sin_tt = sin_sb[:, tt % POS_TILES, :].unsqueeze(1).to_broadcast([P, 2, W])
            a = first.tile([P, 2, W], F32, name="a")
            b = second.tile([P, 2, W], F32, name="b")
            nc.vector.tensor_tensor(out=a[:], in0=both[:], in1=cos_tt, op=MULT)
            finish_head0()
            nc.vector.tensor_tensor(out=b[:], in0=both[:], in1=sin_tt, op=MULT)
            finish_head1()
            waiting.append((a, b, tt, cb, m))

        nc.gpsimd.memset(zero[:], 0.0)
        for i in range(len(SCALE_GROUPS)):
            nc.vector.memset(w0_planes[i][2][:].bitcast(I32), 0)
            nc.vector.memset(x_planes[i][2][:].bitcast(I32), 0)
        for wc, ws in ring:
            nc.vector.memset(ws[:].bitcast(I32), 0)
        def load_start_codes(i, c0, c1):
            g0, g1, wc = w0_codes[i]
            xc = x_codes[i][2]
            if c0 == 0:
                load_codes(nc, g0, g1, wc[:], wq_words, 0, W)
            load_codes(nc, g0, g1, xc[:, :, 2 * c0 : 2 * c1], x_words, c0, c1 - c0)

        def load_start_scales(i):
            g0, g1, ws = w0_planes[i]
            load_scales(nc, g0, g1, ws, wq_scales, 0, W)
            load_scales(nc, g0, g1, x_planes[i][2], x_scales, 0, TOKENS)

        load_start_codes(0, 0, HEAD_TOKENS)
        load_start_scales(0)
        load_start_codes(0, HEAD_TOKENS, TOKENS)
        load_start_codes(1, 0, TOKENS)
        load_start_scales(1)
        load_start_codes(2, 0, TOKENS)
        load_start_scales(2)
        load_start_codes(3, 0, TOKENS)
        load_tables(0)
        for piece in range(1, 4):
            load_piece(piece)

        warm = bank(BANKS - 1)
        for i in range(WARMUP):
            nc.tensor.matmul(out=warm[:, 0:P], lhsT=zero[:], rhs=zero[:], start=True, stop=True)

        accs = []
        for tt in range(TOKEN_TILES):
            accs.append(bank(tt))
        for g in range(PASSES):
            for tt in range(TOKEN_TILES):
                mx(accs[tt], W, tt, 0, g)
        pairs = []
        for tt in range(TOKEN_TILES):
            both = heads.tile([P, 2, W], F32, name="both")
            nc.scalar.copy(out=both[:, 0, :], in_=accs[tt][:])
            pairs.append(both)
        for tt in range(TOKEN_TILES):
            acc = bank(tt)
            for g in range(PASSES):
                mx(acc, W, tt, 1, g)
            nc.scalar.copy(out=pairs[tt][:, 1, :], in_=acc[:])
            rotate(pairs[tt], tt, 0, 0)
            if 4 + tt // 2 <= RING and tt % 2 == 1:
                load_piece(4 + tt // 2)
        load_tables(1)

        slot = 0
        for u in range(1, len(units)):
            cb, m = units[u]
            for piece in (2 * u + RING - 2, 2 * u + RING - 1):
                if RING < piece < 2 * len(units):
                    load_piece(piece)
            if m == 0 and cb + 1 == 2:
                load_tables(2)
            for tt in range(TOKEN_TILES):
                last = u == len(units) - 1 and tt == TOKEN_TILES - 1
                if u < len(units) - 1 or tt < TOKEN_TILES - DIRECT:
                    both = heads.tile([P, 2, W], F32, name="both")
                    for h in range(2):
                        acc = bank(slot + h)
                        for g in range(PASSES):
                            mx(acc, W, tt, 2 * u + h, g)
                        nc.scalar.copy(out=both[:, h, :], in_=acc[:])
                    rotate(both, tt, cb, m)
                    slot += 2
                    continue
                finish_head0()
                finish_head1()
                c0 = 0
                for width in TAIL_WIDTHS if last else (W,):
                    acc0 = bank(slot)
                    for g in range(PASSES):
                        mx(acc0, width, tt, 2 * u, g, c0)
                    a = head0_products(acc0, width, tt, cb, c0)
                    acc1 = bank(slot + 1)
                    for g in range(PASSES):
                        mx(acc1, width, tt, 2 * u + 1, g, c0)
                    b = head1_products(acc1, width, tt, cb, c0)
                    end = last and c0 >= TAIL_WIDTHS[0]
                    add_and_store(nc.vector if end else nc.gpsimd, a, b, width, tt, cb, m, c0)
                    slot += 2
                    c0 += width
